import numpy as np
import ml_dtypes


def mxq(x, axis, fmt="e4m3"):
    dtype, down = {"e4m3": (ml_dtypes.float8_e4m3fn, 7), "e5m2": (ml_dtypes.float8_e5m2, 14)}[fmt]
    v = np.moveaxis(np.asarray(x, np.float32).astype(ml_dtypes.bfloat16).astype(np.float64), axis, -1)
    blocks = v.reshape(v.shape[:-1] + (-1, 32))
    amax = np.abs(blocks).max(-1, keepdims=True)
    byte = np.maximum(np.where(amax > 0, np.frexp(amax)[1] - 1 + 127, 0) - down, 1)
    scale = np.exp2(byte - 127.0)
    codes = (blocks / scale).astype(np.float32).astype(dtype).astype(np.float64)
    return np.moveaxis((codes * scale).reshape(v.shape), -1, axis)


WIDE = False


def mx_kscale(k):
    if not WIDE:
        return np.ones(k)
    levels = np.array([10, -10, 5, -5, 0])
    if k % 512:
        return np.exp2(np.random.permutation(np.resize(levels, k // 32))).repeat(32)
    a = np.empty((k // 512, 16))
    for p in range(k // 512):
        a[p, :8] = np.random.permutation(np.resize(levels, 8))
        for g in range(8):
            far = levels[np.abs(levels - a[p, g]) >= 10]
            a[p, g + 8] = far[np.random.randint(len(far))]
    return np.exp2(a.ravel()).repeat(32)


BF16 = ml_dtypes.bfloat16


def bf(x):
    return np.asarray(x, np.float32).astype(BF16)


def f64(x):
    return np.asarray(x).astype(np.float64)


B, T, D, H = 2, 1024, 512, 2048
R = B * T
EPS = 1e-5


def sigmoid(v):
    return 1.0 / (1.0 + np.exp(-v))


def layer_norm(x, g, b):
    mu = x.mean(-1, keepdims=True)
    var = np.square(x - mu).mean(-1, keepdims=True)
    return (x - mu) / np.sqrt(var + EPS) * g + b


def setup_inputs():
    s, t = mx_kscale(D), mx_kscale(D)
    n = np.random.standard_normal
    return {"x": bf(n((B, T, D))), "yt": bf(n((B, T, D)) * 0.5 * t),
            "ln1_g": bf((1.0 + 0.2 * n(D)) * s), "ln1_b": bf(0.3 * n(D) * s),
            "Wq": bf(n((D, D)) * 1.5 / np.sqrt(D) / s[:, None]), "bq": bf(0.3 * n(D)),
            "Wo": bf(n((D, D)) * 2.5 / np.sqrt(D) / t[:, None]), "bo": bf(0.3 * n(D))}


def reference(x, yt, ln1_g, ln1_b, Wq, bq, Wo, bo):
    xr = f64(x).reshape(R, D)
    h = layer_norm(xr, f64(ln1_g), f64(ln1_b))
    q = (mxq(h, 1, "e4m3") @ mxq(f64(Wq), 0, "e4m3")) + f64(bq)
    y = sigmoid(q) * f64(yt).reshape(R, D)
    attn = (mxq(y, 1, "e4m3") @ mxq(f64(Wo), 0, "e4m3")) + f64(bo)
    return (attn + xr).reshape(B, T, D)

@@ -1,0 +1,284 @@
+import concourse.mybir as mybir
+from concourse.masks import make_identity
+
+F32 = mybir.dt.float32
+BF16 = mybir.dt.bfloat16
+U32 = mybir.dt.uint32
+U8 = mybir.dt.uint8
+FP8X4 = mybir.dt.float8_e4m3fn_x4
+ALU = mybir.AluOpType
+ACT = mybir.ActivationFunctionType
+
+P = 128
+PACK = 4
+D = P * PACK
+ROWS = 2048
+TILES = ROWS // P
+CHUNK_TILES = 2
+CHUNK_ROWS = CHUNK_TILES * P
+CHUNKS = TILES // CHUNK_TILES
+STATS_AHEAD = 5
+VEC_PAD = 16
+RUN = 4
+EPS = 1e-5
+
+FLOPS = 2 * 2 * ROWS * D * D
+
+
+def tile_attentionfreetransformerencoder_pb_kernel(tc, x, yt, ln1_g, ln1_b, Wq, bq, Wo, bo, out):
+    nc = tc.nc
+    x_view = x.flatten_outer_dims().rearrange("(p t) d -> p t d", t=TILES)
+    yt_view = yt.flatten_outer_dims().rearrange("(p t) d -> p t d", t=TILES)
+    out_view = out.flatten_outer_dims().rearrange("(p t) d -> p t d", t=TILES)
+
+    with (
+        tc.tile_pool(name="consts", bufs=1) as consts,
+        tc.tile_pool(name="resident", bufs=1) as resident,
+        tc.tile_pool(name="work", bufs=3) as work,
+        tc.psum_pool(name="psum", bufs=2) as psum,
+        tc.manual_schedule(),
+    ):
+        x_sb = [resident.tile([P, CHUNK_TILES, D], BF16, name="x%d" % c) for c in range(CHUNKS)]
+        yt_sb = [resident.tile([P, CHUNK_TILES, D], BF16, name="yt%d" % c) for c in range(CHUNKS)]
+        wq_raw = consts.tile([P, PACK, D], BF16, name="wq_raw")
+        wo_raw = consts.tile([P, PACK, D], BF16, name="wo_raw")
+        vec_raw = consts.tile([P, 3, VEC_PAD], BF16, name="vec_raw")
+        bo_all = consts.tile([P, D], BF16, name="bo_all")
+
+        def load_chunk(dst, view, c):
+            nc.sync.dma_start(out=dst[c][:], in_=view[:, c * CHUNK_TILES : (c + 1) * CHUNK_TILES, :])
+
+        def load_weight(dst, w):
+            nc.sync.dma_start(out=dst[:], in_=w.rearrange("(p j) n -> p j n", j=PACK))
+
+        load_chunk(x_sb, x_view, 0)
+        for i, vec in enumerate((ln1_g, ln1_b, bq)):
+            nc.sync.dma_start(out=vec_raw[:, i, 0:PACK], in_=vec.rearrange("(p j) -> p j", j=PACK))
+        load_weight(wq_raw, Wq)
+        load_chunk(x_sb, x_view, 1)
+        load_chunk(x_sb, x_view, 2)
+        load_weight(wo_raw, Wo)
+        for c in range(3, CHUNKS):
+            load_chunk(x_sb, x_view, c)
+            load_chunk(yt_sb, yt_view, c - 3)
+        nc.sync.dma_start(out=bo_all[:], in_=bo.partition_broadcast(P))
+        for c in range(CHUNKS - 3, CHUNKS):
+            load_chunk(yt_sb, yt_view, c)
+
+        warm = consts.tile([P, 1], F32, name="warm")
+        nc.vector.memset(warm[:], 0.0)
+        warm_out = consts.tile([P, 1], F32, name="warm_out")
+        nc.scalar.activation(out=warm_out[:], in_=warm[:], func=ACT.Sigmoid)
+
+        ident_f32 = consts.tile([P, P], F32, name="ident_f32")
+        make_identity(nc, ident_f32[:])
+        neg_half = consts.tile([P, CHUNK_TILES], F32, name="neg_half")
+        nc.gpsimd.memset(neg_half[:], -0.5)
+
+        wq_grouped = consts.tile([P, D, PACK], BF16, name="wq_grouped", align_bytes=64)
+        wo_grouped = consts.tile([P, D, PACK], BF16, name="wo_grouped", align_bytes=64)
+        wq_codes = consts.tile([P, D], U32, name="wq_codes", align_bytes=64)
+        wq_scales = consts.tile([P, D], U8, name="wq_scales", align_bytes=64)
+        wo_codes = consts.tile([P, D], U32, name="wo_codes", align_bytes=64)
+        wo_scales = consts.tile([P, D], U8, name="wo_scales", align_bytes=64)
+        cols = consts.tile([P, 3 * PACK], F32, name="cols")
+        g_col = cols[:, 0:PACK]
+        b_col = cols[:, PACK : 2 * PACK]
+        bq_col = cols[:, 2 * PACK : 3 * PACK]
+
+        rstd, shift, xn, xnT, hT, h_grouped, h_codes, h_scales = {}, {}, {}, {}, {}, {}, {}, {}
+        qT, gate, ytT, y_grouped, y_codes, y_scales, o, res = {}, {}, {}, {}, {}, {}, {}, {}
+
+        def regroup(copy, grouped, planes):
+            copy(
+                out=grouped[:].rearrange("p (c i) j -> p c j i", i=RUN),
+                in_=planes[:].rearrange("p j (c i) -> p c j i", i=RUN),
+            )
+
+        def regroup_wq(copy, grouped, planes):
+            copy(
+                out=grouped[:].rearrange("p (t m) j -> p t m j", t=PACK),
+                in_=planes[:].rearrange("p j (m t) -> p t m j", t=PACK),
+            )
+
+        def quantise(grouped, codes, scales):
+            nc.vector.quantize_mx(
+                out=codes[:].bitcast(FP8X4), scales=scales[:], in_=grouped[:].rearrange("p w j -> p (w j)")
+            )
+
+        def stats(c):
+            bn = work.tile([P, CHUNK_TILES, 6], F32, name="bn")
+            mean_var = work.tile([P, CHUNK_TILES, 2], F32, name="mean_var")
+            for i in range(CHUNK_TILES):
+                nc.vector.bn_stats(out=bn[:, i, :], in_=x_sb[c][:, i, :])
+            for i in range(CHUNK_TILES):
+                nc.vector.bn_aggr(out=mean_var[:, i, :], in_=bn[:, i, :])
+            var_eps = work.tile([P, CHUNK_TILES], F32, name="var_eps")
+            nc.gpsimd.tensor_scalar(
+                out=var_eps[:], in0=mean_var[:, :, 1], scalar1=EPS, scalar2=None, op0=ALU.add
+            )
+            neg_mean = work.tile([P, CHUNK_TILES], F32, name="neg_mean")
+            nc.gpsimd.tensor_scalar(
+                out=neg_mean[:], in0=mean_var[:, :, 0], scalar1=-1.0, scalar2=None, op0=ALU.mult
+            )
+            rstd[c] = resident.tile([P, CHUNK_TILES], F32, name="rstd%d" % c)
+            nc.gpsimd.tensor_tensor(out=rstd[c][:], in0=var_eps[:], in1=neg_half[:], op=ALU.pow)
+            shift[c] = resident.tile([P, CHUNK_TILES], F32, name="shift%d" % c)
+            nc.gpsimd.tensor_tensor(out=shift[c][:], in0=neg_mean[:], in1=rstd[c][:], op=ALU.mult)
+
+        def normalise(c):
+            xn[c] = work.tile([P, CHUNK_TILES, PACK, P], F32, name="xn")
+            for i in range(CHUNK_TILES):
+                nc.scalar.activation(
+                    out=xn[c][:, i, :, :],
+                    in_=x_sb[c][:, i, :].rearrange("p (m j) -> p j m", j=PACK),
+                    func=ACT.Identity,
+                    scale=rstd[c][:, i : i + 1],
+                    bias=shift[c][:, i : i + 1],
+                )
+
+        def transpose_x(c):
+            xnT[c] = []
+            for b in range(2):
+                bank = psum.tile([P, 2, CHUNK_ROWS], F32, name="xnT")
+                for jj in range(2):
+                    j = 2 * b + jj
+                    for i in range(CHUNK_TILES):
+                        nc.tensor.transpose(
+                            bank[:, jj, i * P : (i + 1) * P], xn[c][:, i, j, :], ident_f32[:]
+                        )
+                xnT[c].append(bank)
+
+        def gain_shift(c):
+            hT[c] = work.tile([P, PACK, CHUNK_ROWS], BF16, name="hT")
+            for j in range(PACK):
+                nc.scalar.activation(
+                    out=hT[c][:, j, :],
+                    in_=xnT[c][j // 2][:, j % 2, :],
+                    func=ACT.Identity,
+                    scale=g_col[:, j : j + 1],
+                    bias=b_col[:, j : j + 1],
+                )
+
+        def group_h(c):
+            h_grouped[c] = work.tile([P, CHUNK_ROWS, PACK], BF16, name="h_grouped", align_bytes=64)
+            regroup(nc.vector.tensor_copy if c % 2 == 0 else nc.scalar.copy, h_grouped[c], hT[c])
+
+        def quantise_h(c):
+            h_codes[c] = work.tile([P, CHUNK_ROWS], U32, name="h_codes", align_bytes=64)
+            h_scales[c] = work.tile([P, CHUNK_ROWS], U8, name="h_scales", align_bytes=64)
+            quantise(h_grouped[c], h_codes[c], h_scales[c])
+
+        def q_matmuls(c):
+            qT[c] = []
+            for b in range(2):
+                bank = psum.tile([P, 2, CHUNK_ROWS], F32, name="qT")
+                for jj in range(2):
+                    j = 2 * b + jj
+                    nc.tensor.matmul_mx(
+                        out=bank[:, jj, :],
+                        lhsT=wq_codes[:, j * P : (j + 1) * P].bitcast(FP8X4),
+                        lhsT_scale=wq_scales[:, j * P : (j + 1) * P],
+                        rhs=h_codes[c][:].bitcast(FP8X4),
+                        rhs_scale=h_scales[c][:],
+                        start=True,
+                        stop=True,
+                    )
+                qT[c].append(bank)
+
+        def sigmoid(c):
+            gate[c] = work.tile([P, PACK, CHUNK_ROWS], F32, name="gate")
+            for j in range(PACK):
+                nc.scalar.activation(
+                    out=gate[c][:, j, :],
+                    in_=qT[c][j // 2][:, j % 2, :],
+                    func=ACT.Sigmoid,
+                    bias=bq_col[:, j : j + 1],
+                )
+
+        def transpose_yt(c):
+            ytT[c] = psum.tile([P, 2, CHUNK_ROWS], F32, name="ytT")
+            for i in range(CHUNK_TILES):
+                words = yt_sb[c][:, i, :].bitcast(F32)
+                for u in range(2):
+                    nc.tensor.transpose(ytT[c][:, u, i * P : (i + 1) * P], words[:, u::2], ident_f32[:])
+
+        def product(c):
+            y_grouped[c] = work.tile([P, CHUNK_ROWS, PACK], BF16, name="y_grouped", align_bytes=64)
+            nc.vector.tensor_tensor(
+                out=y_grouped[c][:].rearrange("p w (u e) -> p w u e", e=2),
+                in0=ytT[c][:].bitcast(BF16).rearrange("p u (w e) -> p w u e", e=2),
+                in1=gate[c][:].rearrange("p (u e) w -> p w u e", e=2),
+                op=ALU.mult,
+            )
+
+        def quantise_y(c):
+            y_codes[c] = work.tile([P, CHUNK_ROWS], U32, name="y_codes", align_bytes=64)
+            y_scales[c] = work.tile([P, CHUNK_ROWS], U8, name="y_scales", align_bytes=64)
+            quantise(y_grouped[c], y_codes[c], y_scales[c])
+
+        def out_matmuls(c):
+            o[c] = []
+            for i in range(CHUNK_TILES):
+                bank = psum.tile([P, D], F32, name="o")
+                nc.tensor.matmul_mx(
+                    out=bank[:],
+                    lhsT=y_codes[c][:, i * P : (i + 1) * P].bitcast(FP8X4),
+                    lhsT_scale=y_scales[c][:, i * P : (i + 1) * P],
+                    rhs=wo_codes[:].bitcast(FP8X4),
+                    rhs_scale=wo_scales[:],
+                    start=True,
+                    stop=True,
+                )
+                o[c].append(bank)
+
+        def residual(c):
+            res[c] = resident.tile([P, CHUNK_TILES, D], F32, name="res%d" % c)
+            nc.vector.tensor_tensor(
+                out=res[c][:],
+                in0=x_sb[c][:],
+                in1=bo_all[:].unsqueeze(1).to_broadcast([P, CHUNK_TILES, D]),
+                op=ALU.add,
+            )
+
+        def add_store(c, i):
+            nc.vector.tensor_tensor(out=res[c][:, i, :], in0=o[c][i][:], in1=res[c][:, i, :], op=ALU.add)
+            nc.sync.dma_start(out=out_view[:, c * CHUNK_TILES + i, :], in_=res[c][:, i, :])
+
+        def add_first(c):
+            add_store(c, 0)
+
+        def add_second(c):
+            add_store(c, 1)
+
+        def run(stage, c):
+            if 0 <= c < CHUNKS:
+                stage(c)
+
+        regroup_wq(nc.scalar.copy, wq_grouped, wq_raw)
+        for c in range(STATS_AHEAD):
+            stats(c)
+        nc.scalar.copy(out=cols[:].rearrange("p (i j) -> p i j", j=PACK), in_=vec_raw[:, :, 0:PACK])
+        normalise(0)
+        normalise(1)
+        transpose_x(0)
+        regroup(nc.vector.tensor_copy, wo_grouped, wo_raw)
+        quantise(wq_grouped, wq_codes, wq_scales)
+        quantise(wo_grouped, wo_codes, wo_scales)
+
+        for s in range(CHUNKS + 2):
+            run(gain_shift, s)
+            run(group_h, s)
+            run(sigmoid, s - 1)
+            run(normalise, s + 2)
+            run(transpose_x, s + 1)
+            run(transpose_yt, s)
+            run(add_first, s - 2)
+            run(quantise_h, s)
+            run(q_matmuls, s)
+            run(product, s - 1)
+            run(add_second, s - 2)
+            run(quantise_y, s - 1)
+            run(out_matmuls, s - 1)
+            run(stats, s + STATS_AHEAD)
+            run(residual, s)

@@ -70,6 +70,8 @@ def tile_attentionfreetransformerencoder_pb_kernel(tc, x, yt, ln1_g, ln1_b, Wq, 
         warm_out = consts.tile([P, 1], F32, name="warm_out")
         nc.scalar.activation(out=warm_out[:], in_=warm[:], func=ACT.Sigmoid)
 
+        ident_bf16 = consts.tile([P, P], BF16, name="ident_bf16")
+        make_identity(nc, ident_bf16[:])
         ident_f32 = consts.tile([P, P], F32, name="ident_f32")
         make_identity(nc, ident_f32[:])
         neg_half = consts.tile([P, CHUNK_TILES], F32, name="neg_half")
@@ -197,18 +199,17 @@ def tile_attentionfreetransformerencoder_pb_kernel(tc, x, yt, ln1_g, ln1_b, Wq, 
                 )
 
         def transpose_yt(c):
-            ytT[c] = psum.tile([P, 2, CHUNK_ROWS], F32, name="ytT")
-            for i in range(CHUNK_TILES):
-                words = yt_sb[c][:, i, :].bitcast(F32)
-                for u in range(2):
-                    nc.tensor.transpose(ytT[c][:, u, i * P : (i + 1) * P], words[:, u::2], ident_f32[:])
+            ytT[c] = psum.tile([P, PACK, CHUNK_ROWS], BF16, name="ytT")
+            for j in range(PACK):
+                for i in range(CHUNK_TILES):
+                    nc.tensor.transpose(ytT[c][:, j, i * P : (i + 1) * P], yt_sb[c][:, i, j::PACK], ident_bf16[:])
 
         def product(c):
             y_grouped[c] = work.tile([P, CHUNK_ROWS, PACK], BF16, name="y_grouped", align_bytes=64)
             nc.vector.tensor_tensor(
-                out=y_grouped[c][:].rearrange("p w (u e) -> p w u e", e=2),
-                in0=ytT[c][:].bitcast(BF16).rearrange("p u (w e) -> p w u e", e=2),
-                in1=gate[c][:].rearrange("p (u e) w -> p w u e", e=2),
+                out=y_grouped[c][:].rearrange("p (c i) j -> p c j i", i=RUN),
+                in0=ytT[c][:].rearrange("p j (c i) -> p c j i", i=RUN),
+                in1=gate[c][:].rearrange("p j (c i) -> p c j i", i=RUN),
                 op=ALU.mult,
             )
 

@@ -19,6 +19,7 @@ CHUNK_ROWS = CHUNK_TILES * P
 CHUNKS = TILES // CHUNK_TILES
 STATS_AHEAD = 5
 VEC_PAD = 16
+VECTOR_GROUPS = (0, 2)
 RUN = 4
 EPS = 1e-5
 
@@ -104,22 +105,23 @@ def tile_attentionfreetransformerencoder_pb_kernel(tc, x, yt, ln1_g, ln1_b, Wq, 
             )
 
         def quantise(grouped, codes, scales):
-            nc.vector.quantize_mx(
-                out=codes[:].bitcast(FP8X4), scales=scales[:], in_=grouped[:].rearrange("p w j -> p (w j)")
-            )
+            nc.vector.quantize_mx(out=codes.bitcast(FP8X4), scales=scales, in_=grouped.rearrange("p w j -> p (w j)"))
+
+        def part(c, i):
+            return slice(i * P, (i + 1) * P) if c == CHUNKS - 1 else slice(0, CHUNK_ROWS)
 
         def stats(c):
-            bn = work.tile([P, CHUNK_TILES, 6], F32, name="bn")
-            mean_var = work.tile([P, CHUNK_TILES, 2], F32, name="mean_var")
+            bn = resident.tile([P, CHUNK_TILES, 6], F32, name="bn%d" % c)
+            mean_var = resident.tile([P, CHUNK_TILES, 2], F32, name="mean_var%d" % c)
             for i in range(CHUNK_TILES):
                 nc.vector.bn_stats(out=bn[:, i, :], in_=x_sb[c][:, i, :])
             for i in range(CHUNK_TILES):
                 nc.vector.bn_aggr(out=mean_var[:, i, :], in_=bn[:, i, :])
-            var_eps = work.tile([P, CHUNK_TILES], F32, name="var_eps")
+            var_eps = resident.tile([P, CHUNK_TILES], F32, name="var_eps%d" % c)
             nc.gpsimd.tensor_scalar(
                 out=var_eps[:], in0=mean_var[:, :, 1], scalar1=EPS, scalar2=None, op0=ALU.add
             )
-            neg_mean = work.tile([P, CHUNK_TILES], F32, name="neg_mean")
+            neg_mean = resident.tile([P, CHUNK_TILES], F32, name="neg_mean%d" % c)
             nc.gpsimd.tensor_scalar(
                 out=neg_mean[:], in0=mean_var[:, :, 0], scalar1=-1.0, scalar2=None, op0=ALU.mult
             )
@@ -164,12 +166,12 @@ def tile_attentionfreetransformerencoder_pb_kernel(tc, x, yt, ln1_g, ln1_b, Wq, 
 
         def group_h(c):
             h_grouped[c] = work.tile([P, CHUNK_ROWS, PACK], BF16, name="h_grouped", align_bytes=64)
-            regroup(nc.vector.tensor_copy if c % 2 == 0 else nc.scalar.copy, h_grouped[c], hT[c])
+            regroup(nc.vector.tensor_copy if c in VECTOR_GROUPS else nc.scalar.copy, h_grouped[c], hT[c])
 
         def quantise_h(c):
             h_codes[c] = work.tile([P, CHUNK_ROWS], U32, name="h_codes", align_bytes=64)
             h_scales[c] = work.tile([P, CHUNK_ROWS], U8, name="h_scales", align_bytes=64)
-            quantise(h_grouped[c], h_codes[c], h_scales[c])
+            quantise(h_grouped[c][:], h_codes[c][:], h_scales[c][:])
 
         def q_matmuls(c):
             qT[c] = []
@@ -204,34 +206,38 @@ def tile_attentionfreetransformerencoder_pb_kernel(tc, x, yt, ln1_g, ln1_b, Wq, 
                 for i in range(CHUNK_TILES):
                     nc.tensor.transpose(ytT[c][:, j, i * P : (i + 1) * P], yt_sb[c][:, i, j::PACK], ident_bf16[:])
 
-        def product(c):
-            y_grouped[c] = work.tile([P, CHUNK_ROWS, PACK], BF16, name="y_grouped", align_bytes=64)
+        def product(c, i):
+            if i == 0:
+                y_grouped[c] = work.tile([P, CHUNK_ROWS, PACK], BF16, name="y_grouped", align_bytes=64)
+            w = part(c, i)
             nc.vector.tensor_tensor(
-                out=y_grouped[c][:].rearrange("p (c i) j -> p c j i", i=RUN),
-                in0=ytT[c][:].rearrange("p j (c i) -> p c j i", i=RUN),
-                in1=gate[c][:].rearrange("p j (c i) -> p c j i", i=RUN),
+                out=y_grouped[c][:, w, :].rearrange("p (c i) j -> p c j i", i=RUN),
+                in0=ytT[c][:, :, w].rearrange("p j (c i) -> p c j i", i=RUN),
+                in1=gate[c][:, :, w].rearrange("p j (c i) -> p c j i", i=RUN),
                 op=ALU.mult,
             )
 
-        def quantise_y(c):
-            y_codes[c] = work.tile([P, CHUNK_ROWS], U32, name="y_codes", align_bytes=64)
-            y_scales[c] = work.tile([P, CHUNK_ROWS], U8, name="y_scales", align_bytes=64)
-            quantise(y_grouped[c], y_codes[c], y_scales[c])
+        def quantise_y(c, i):
+            if i == 0:
+                y_codes[c] = work.tile([P, CHUNK_ROWS], U32, name="y_codes", align_bytes=64)
+                y_scales[c] = work.tile([P, CHUNK_ROWS], U8, name="y_scales", align_bytes=64)
+            w = part(c, i)
+            quantise(y_grouped[c][:, w, :], y_codes[c][:, w], y_scales[c][:, w])
 
-        def out_matmuls(c):
-            o[c] = []
-            for i in range(CHUNK_TILES):
-                bank = psum.tile([P, D], F32, name="o")
-                nc.tensor.matmul_mx(
-                    out=bank[:],
-                    lhsT=y_codes[c][:, i * P : (i + 1) * P].bitcast(FP8X4),
-                    lhsT_scale=y_scales[c][:, i * P : (i + 1) * P],
-                    rhs=wo_codes[:].bitcast(FP8X4),
-                    rhs_scale=wo_scales[:],
-                    start=True,
-                    stop=True,
-                )
-                o[c].append(bank)
+        def out_matmul(c, i):
+            if i == 0:
+                o[c] = []
+            bank = psum.tile([P, D], F32, name="o")
+            nc.tensor.matmul_mx(
+                out=bank[:],
+                lhsT=y_codes[c][:, i * P : (i + 1) * P].bitcast(FP8X4),
+                lhsT_scale=y_scales[c][:, i * P : (i + 1) * P],
+                rhs=wo_codes[:].bitcast(FP8X4),
+                rhs_scale=wo_scales[:],
+                start=True,
+                stop=True,
+            )
+            o[c].append(bank)
 
         def residual(c):
             res[c] = resident.tile([P, CHUNK_TILES, D], F32, name="res%d" % c)
@@ -246,15 +252,9 @@ def tile_attentionfreetransformerencoder_pb_kernel(tc, x, yt, ln1_g, ln1_b, Wq, 
             nc.vector.tensor_tensor(out=res[c][:, i, :], in0=o[c][i][:], in1=res[c][:, i, :], op=ALU.add)
             nc.sync.dma_start(out=out_view[:, c * CHUNK_TILES + i, :], in_=res[c][:, i, :])
 
-        def add_first(c):
-            add_store(c, 0)
-
-        def add_second(c):
-            add_store(c, 1)
-
-        def run(stage, c):
+        def run(stage, c, *i):
             if 0 <= c < CHUNKS:
-                stage(c)
+                stage(c, *i)
 
         regroup_wq(nc.scalar.copy, wq_grouped, wq_raw)
         for c in range(STATS_AHEAD):
@@ -264,22 +264,32 @@ def tile_attentionfreetransformerencoder_pb_kernel(tc, x, yt, ln1_g, ln1_b, Wq, 
         normalise(1)
         transpose_x(0)
         regroup(nc.vector.tensor_copy, wo_grouped, wo_raw)
-        quantise(wq_grouped, wq_codes, wq_scales)
-        quantise(wo_grouped, wo_codes, wo_scales)
+        quantise(wq_grouped[:], wq_codes[:], wq_scales[:])
+        quantise(wo_grouped[:], wo_codes[:], wo_scales[:])
 
         for s in range(CHUNKS + 2):
             run(gain_shift, s)
+            run(normalise, s + 2)
             run(group_h, s)
             run(sigmoid, s - 1)
-            run(normalise, s + 2)
             run(transpose_x, s + 1)
             run(transpose_yt, s)
-            run(add_first, s - 2)
+            if s - 2 < CHUNKS - 1:
+                run(out_matmul, s - 2, 0)
+                run(out_matmul, s - 2, 1)
+            run(residual, s - 1)
             run(quantise_h, s)
             run(q_matmuls, s)
-            run(product, s - 1)
-            run(add_second, s - 2)
-            run(quantise_y, s - 1)
-            run(out_matmuls, s - 1)
             run(stats, s + STATS_AHEAD)
-            run(residual, s)
+            run(add_store, s - 2, 0)
+            run(product, s - 1, 0)
+            if s - 1 == CHUNKS - 1:
+                product(s - 1, 1)
+                quantise_y(s - 1, 0)
+                out_matmul(s - 1, 0)
+            run(add_store, s - 2, 1)
+            if s - 1 == CHUNKS - 1:
+                quantise_y(s - 1, 1)
+                out_matmul(s - 1, 1)
+            else:
+                run(quantise_y, s - 1, 0)

@@ -44,7 +44,8 @@ def tile_attentionfreetransformerencoder_pb_kernel(tc, x, yt, ln1_g, ln1_b, Wq, 
         wq_raw = consts.tile([P, PACK, D], BF16, name="wq_raw")
         wo_raw = consts.tile([P, PACK, D], BF16, name="wo_raw")
         vec_raw = consts.tile([P, 3, VEC_PAD], BF16, name="vec_raw")
-        bo_all = consts.tile([P, D], BF16, name="bo_all")
+        bo_row = consts.tile([P, D], BF16, name="bo_row")
+        bo_all = consts.tile([P, D], F32, name="bo_all")
 
         def load_chunk(dst, view, c):
             nc.sync.dma_start(out=dst[c][:], in_=view[:, c * CHUNK_TILES : (c + 1) * CHUNK_TILES, :])
@@ -52,17 +53,18 @@ def tile_attentionfreetransformerencoder_pb_kernel(tc, x, yt, ln1_g, ln1_b, Wq, 
         def load_weight(dst, w):
             nc.sync.dma_start(out=dst[:], in_=w.rearrange("(p j) n -> p j n", j=PACK))
 
+        nc.vector.memset(bo_row[:], 0.0)
         load_chunk(x_sb, x_view, 0)
+        load_chunk(x_sb, x_view, 1)
+        nc.sync.dma_start(out=bo_row[0:1, :], in_=bo.unsqueeze(0))
         for i, vec in enumerate((ln1_g, ln1_b, bq)):
             nc.sync.dma_start(out=vec_raw[:, i, 0:PACK], in_=vec.rearrange("(p j) -> p j", j=PACK))
         load_weight(wq_raw, Wq)
-        load_chunk(x_sb, x_view, 1)
         load_chunk(x_sb, x_view, 2)
         load_weight(wo_raw, Wo)
         for c in range(3, CHUNKS):
             load_chunk(x_sb, x_view, c)
             load_chunk(yt_sb, yt_view, c - 3)
-        nc.sync.dma_start(out=bo_all[:], in_=bo.partition_broadcast(P))
         for c in range(CHUNKS - 3, CHUNKS):
             load_chunk(yt_sb, yt_view, c)
 
@@ -75,6 +77,8 @@ def tile_attentionfreetransformerencoder_pb_kernel(tc, x, yt, ln1_g, ln1_b, Wq, 
         make_identity(nc, ident_bf16[:])
         ident_f32 = consts.tile([P, P], F32, name="ident_f32")
         make_identity(nc, ident_f32[:])
+        ones_bf16 = consts.tile([P, P], BF16, name="ones_bf16")
+        nc.gpsimd.memset(ones_bf16[:], 1.0)
         neg_half = consts.tile([P, CHUNK_TILES], F32, name="neg_half")
         nc.gpsimd.memset(neg_half[:], -0.5)
 
@@ -256,13 +260,16 @@ def tile_attentionfreetransformerencoder_pb_kernel(tc, x, yt, ln1_g, ln1_b, Wq, 
             if 0 <= c < CHUNKS:
                 stage(c, *i)
 
-        regroup_wq(nc.scalar.copy, wq_grouped, wq_raw)
         for c in range(STATS_AHEAD):
             stats(c)
+        bo_bank = psum.tile([P, D], F32, name="bo_bank", tag="o")
+        nc.tensor.matmul(bo_bank[:], ones_bf16[:], bo_row[:], start=True, stop=True)
+        nc.scalar.copy(out=bo_all[:], in_=bo_bank[:])
         nc.scalar.copy(out=cols[:].rearrange("p (i j) -> p i j", j=PACK), in_=vec_raw[:, :, 0:PACK])
         normalise(0)
-        normalise(1)
         transpose_x(0)
+        regroup_wq(nc.scalar.copy, wq_grouped, wq_raw)
+        normalise(1)
         regroup(nc.vector.tensor_copy, wo_grouped, wo_raw)
         quantise(wq_grouped[:], wq_codes[:], wq_scales[:])
         quantise(wo_grouped[:], wo_codes[:], wo_scales[:])

@@ -17,7 +17,6 @@ TILES = ROWS // P
 CHUNK_TILES = 2
 CHUNK_ROWS = CHUNK_TILES * P
 CHUNKS = TILES // CHUNK_TILES
-STATS_AHEAD = 5
 VEC_PAD = 16
 VECTOR_GROUPS = (0, 2)
 RUN = 4
@@ -61,11 +60,12 @@ def tile_attentionfreetransformerencoder_pb_kernel(tc, x, yt, ln1_g, ln1_b, Wq, 
             nc.sync.dma_start(out=vec_raw[:, i, 0:PACK], in_=vec.rearrange("(p j) -> p j", j=PACK))
         load_weight(wq_raw, Wq)
         load_chunk(x_sb, x_view, 2)
+        load_chunk(x_sb, x_view, 3)
         load_weight(wo_raw, Wo)
-        for c in range(3, CHUNKS):
+        for c in range(4, CHUNKS):
             load_chunk(x_sb, x_view, c)
-            load_chunk(yt_sb, yt_view, c - 3)
-        for c in range(CHUNKS - 3, CHUNKS):
+            load_chunk(yt_sb, yt_view, c - 4)
+        for c in range(CHUNKS - 4, CHUNKS):
             load_chunk(yt_sb, yt_view, c)
 
         warm = consts.tile([P, 1], F32, name="warm")
@@ -79,7 +79,7 @@ def tile_attentionfreetransformerencoder_pb_kernel(tc, x, yt, ln1_g, ln1_b, Wq, 
         make_identity(nc, ident_f32[:])
         ones_bf16 = consts.tile([P, P], BF16, name="ones_bf16")
         nc.gpsimd.memset(ones_bf16[:], 1.0)
-        neg_half = consts.tile([P, CHUNK_TILES], F32, name="neg_half")
+        neg_half = consts.tile([P, TILES], F32, name="neg_half")
         nc.gpsimd.memset(neg_half[:], -0.5)
 
         wq_grouped = consts.tile([P, D, PACK], BF16, name="wq_grouped", align_bytes=64)
@@ -93,7 +93,12 @@ def tile_attentionfreetransformerencoder_pb_kernel(tc, x, yt, ln1_g, ln1_b, Wq, 
         b_col = cols[:, PACK : 2 * PACK]
         bq_col = cols[:, 2 * PACK : 3 * PACK]
 
-        rstd, shift, xn, xnT, hT, h_grouped, h_codes, h_scales = {}, {}, {}, {}, {}, {}, {}, {}
+        mean_var = consts.tile([P, TILES, 2], F32, name="mean_var")
+        var_eps = consts.tile([P, TILES], F32, name="var_eps")
+        rstd = consts.tile([P, TILES], F32, name="rstd")
+        shift = consts.tile([P, TILES], F32, name="shift")
+
+        xn, xnT, hT, h_grouped, h_codes, h_scales = {}, {}, {}, {}, {}, {}
         qT, gate, ytT, y_grouped, y_codes, y_scales, o, res = {}, {}, {}, {}, {}, {}, {}, {}
 
         def regroup(copy, grouped, planes):
@@ -116,23 +121,24 @@ def tile_attentionfreetransformerencoder_pb_kernel(tc, x, yt, ln1_g, ln1_b, Wq, 
 
         def stats(c):
             bn = resident.tile([P, CHUNK_TILES, 6], F32, name="bn%d" % c)
-            mean_var = resident.tile([P, CHUNK_TILES, 2], F32, name="mean_var%d" % c)
             for i in range(CHUNK_TILES):
                 nc.vector.bn_stats(out=bn[:, i, :], in_=x_sb[c][:, i, :])
             for i in range(CHUNK_TILES):
-                nc.vector.bn_aggr(out=mean_var[:, i, :], in_=bn[:, i, :])
-            var_eps = resident.tile([P, CHUNK_TILES], F32, name="var_eps%d" % c)
-            nc.gpsimd.tensor_scalar(
-                out=var_eps[:], in0=mean_var[:, :, 1], scalar1=EPS, scalar2=None, op0=ALU.add
+                nc.vector.bn_aggr(out=mean_var[:, c * CHUNK_TILES + i, :], in_=bn[:, i, :])
+
+        def tiles_of(first, count):
+            return slice(first * CHUNK_TILES, (first + count) * CHUNK_TILES)
+
+        def inverse_deviation(first, count):
+            t = tiles_of(first, count)
+            nc.vector.tensor_scalar(out=var_eps[:, t], in0=mean_var[:, t, 1], scalar1=EPS, scalar2=None, op0=ALU.add)
+            nc.gpsimd.tensor_tensor(out=rstd[:, t], in0=var_eps[:, t], in1=neg_half[:, t], op=ALU.pow)
+
+        def mean_shift(first, count):
+            t = tiles_of(first, count)
+            nc.vector.scalar_tensor_tensor(
+                out=shift[:, t], in0=mean_var[:, t, 0], scalar=-1.0, in1=rstd[:, t], op0=ALU.mult, op1=ALU.mult
             )
-            neg_mean = resident.tile([P, CHUNK_TILES], F32, name="neg_mean%d" % c)
-            nc.gpsimd.tensor_scalar(
-                out=neg_mean[:], in0=mean_var[:, :, 0], scalar1=-1.0, scalar2=None, op0=ALU.mult
-            )
-            rstd[c] = resident.tile([P, CHUNK_TILES], F32, name="rstd%d" % c)
-            nc.gpsimd.tensor_tensor(out=rstd[c][:], in0=var_eps[:], in1=neg_half[:], op=ALU.pow)
-            shift[c] = resident.tile([P, CHUNK_TILES], F32, name="shift%d" % c)
-            nc.gpsimd.tensor_tensor(out=shift[c][:], in0=neg_mean[:], in1=rstd[c][:], op=ALU.mult)
 
         def normalise(c):
             xn[c] = work.tile([P, CHUNK_TILES, PACK, P], F32, name="xn")
@@ -141,8 +147,8 @@ def tile_attentionfreetransformerencoder_pb_kernel(tc, x, yt, ln1_g, ln1_b, Wq, 
                     out=xn[c][:, i, :, :],
                     in_=x_sb[c][:, i, :].rearrange("p (m j) -> p j m", j=PACK),
                     func=ACT.Identity,
-                    scale=rstd[c][:, i : i + 1],
-                    bias=shift[c][:, i : i + 1],
+                    scale=rstd[:, c * CHUNK_TILES + i : c * CHUNK_TILES + i + 1],
+                    bias=shift[:, c * CHUNK_TILES + i : c * CHUNK_TILES + i + 1],
                 )
 
         def transpose_x(c):
@@ -260,18 +266,29 @@ def tile_attentionfreetransformerencoder_pb_kernel(tc, x, yt, ln1_g, ln1_b, Wq, 
             if 0 <= c < CHUNKS:
                 stage(c, *i)
 
-        for c in range(STATS_AHEAD):
-            stats(c)
+        stats(0)
+        inverse_deviation(0, 1)
         bo_bank = psum.tile([P, D], F32, name="bo_bank", tag="o")
         nc.tensor.matmul(bo_bank[:], ones_bf16[:], bo_row[:], start=True, stop=True)
         nc.scalar.copy(out=bo_all[:], in_=bo_bank[:])
         nc.scalar.copy(out=cols[:].rearrange("p (i j) -> p i j", j=PACK), in_=vec_raw[:, :, 0:PACK])
+        stats(1)
+        mean_shift(0, 1)
+        inverse_deviation(1, 1)
         normalise(0)
         transpose_x(0)
         regroup_wq(nc.scalar.copy, wq_grouped, wq_raw)
+        stats(2)
+        stats(3)
+        mean_shift(1, 1)
+        inverse_deviation(2, 2)
         normalise(1)
         regroup(nc.vector.tensor_copy, wo_grouped, wo_raw)
+        stats(4)
+        stats(5)
+        mean_shift(2, 2)
         quantise(wq_grouped[:], wq_codes[:], wq_scales[:])
+        inverse_deviation(4, 2)
         quantise(wo_grouped[:], wo_codes[:], wo_scales[:])
 
         for s in range(CHUNKS + 2):
@@ -287,9 +304,15 @@ def tile_attentionfreetransformerencoder_pb_kernel(tc, x, yt, ln1_g, ln1_b, Wq, 
             run(residual, s - 1)
             run(quantise_h, s)
             run(q_matmuls, s)
-            run(stats, s + STATS_AHEAD)
+            if s == 0:
+                stats(6)
+                stats(7)
+            if s == 1:
+                inverse_deviation(6, 2)
             run(add_store, s - 2, 0)
             run(product, s - 1, 0)
+            if s in (1, 2):
+                mean_shift(2 * s + 2, 2)
             if s - 1 == CHUNKS - 1:
                 product(s - 1, 1)
                 quantise_y(s - 1, 0)

@@ -18,6 +18,7 @@ CHUNK_TILES = 2
 CHUNK_ROWS = CHUNK_TILES * P
 CHUNKS = TILES // CHUNK_TILES
 VEC_PAD = 16
+RES_ON_VECTOR = 6
 VECTOR_GROUPS = (0, 2)
 RUN = 4
 EPS = 1e-5
@@ -99,7 +100,7 @@ def tile_attentionfreetransformerencoder_pb_kernel(tc, x, yt, ln1_g, ln1_b, Wq, 
         shift = consts.tile([P, TILES], F32, name="shift")
 
         xn, xnT, hT, h_grouped, h_codes, h_scales = {}, {}, {}, {}, {}, {}
-        qT, gate, ytT, y_grouped, y_codes, y_scales, o, res = {}, {}, {}, {}, {}, {}, {}, {}
+        qT, gate, ytT, y_grouped, y_codes, y_scales, o, res, res_banks = {}, {}, {}, {}, {}, {}, {}, {}, {}
 
         def regroup(copy, grouped, planes):
             copy(
@@ -249,6 +250,19 @@ def tile_attentionfreetransformerencoder_pb_kernel(tc, x, yt, ln1_g, ln1_b, Wq, 
             )
             o[c].append(bank)
 
+        def residual_on_tensor(c):
+            res_banks[c] = []
+            for i in range(CHUNK_TILES):
+                bank = psum.tile([P, D], F32, name="res_bank", tag="xnT")
+                nc.tensor.matmul(bank[:], ones_bf16[:], bo_row[:], start=True, stop=False)
+                nc.tensor.matmul(bank[:], ident_bf16[:], x_sb[c][:, i, :], start=False, stop=True)
+                res_banks[c].append(bank)
+
+        def copy_residual(c):
+            res[c] = resident.tile([P, CHUNK_TILES, D], F32, name="res%d" % c)
+            for i in range(CHUNK_TILES):
+                nc.scalar.copy(out=res[c][:, i, :], in_=res_banks[c][i][:])
+
         def residual(c):
             res[c] = resident.tile([P, CHUNK_TILES, D], F32, name="res%d" % c)
             nc.vector.tensor_tensor(
@@ -283,40 +297,51 @@ def tile_attentionfreetransformerencoder_pb_kernel(tc, x, yt, ln1_g, ln1_b, Wq, 
         mean_shift(1, 1)
         inverse_deviation(2, 2)
         normalise(1)
+        gain_shift(0)
+        transpose_x(1)
         regroup(nc.vector.tensor_copy, wo_grouped, wo_raw)
         stats(4)
-        stats(5)
         mean_shift(2, 2)
+        normalise(2)
         quantise(wq_grouped[:], wq_codes[:], wq_scales[:])
+        stats(5)
+        group_h(0)
+        quantise_h(0)
+        q_matmuls(0)
+        transpose_yt(0)
         inverse_deviation(4, 2)
         quantise(wo_grouped[:], wo_codes[:], wo_scales[:])
+        stats(6)
+        mean_shift(4, 2)
+        stats(7)
 
-        for s in range(CHUNKS + 2):
+        for s in range(1, CHUNKS + 2):
             run(gain_shift, s)
             run(normalise, s + 2)
             run(group_h, s)
             run(sigmoid, s - 1)
             run(transpose_x, s + 1)
-            run(transpose_yt, s)
+            if CHUNKS - 1 <= s <= CHUNKS:
+                residual_on_tensor(s - 1)
+                copy_residual(s - 1)
             if s - 2 < CHUNKS - 1:
                 run(out_matmul, s - 2, 0)
                 run(out_matmul, s - 2, 1)
-            run(residual, s - 1)
             run(quantise_h, s)
             run(q_matmuls, s)
-            if s == 0:
-                stats(6)
-                stats(7)
+            run(transpose_yt, s)
             if s == 1:
                 inverse_deviation(6, 2)
-            run(add_store, s - 2, 0)
+            if s - 1 < RES_ON_VECTOR:
+                residual(s - 1)
             run(product, s - 1, 0)
-            if s in (1, 2):
-                mean_shift(2 * s + 2, 2)
+            if s == 1:
+                mean_shift(6, 2)
             if s - 1 == CHUNKS - 1:
                 product(s - 1, 1)
                 quantise_y(s - 1, 0)
                 out_matmul(s - 1, 0)
+            run(add_store, s - 2, 0)
             run(add_store, s - 2, 1)
             if s - 1 == CHUNKS - 1:
                 quantise_y(s - 1, 1)

@@ -19,7 +19,7 @@ CHUNK_ROWS = CHUNK_TILES * P
 CHUNKS = TILES // CHUNK_TILES
 VEC_PAD = 16
 RES_ON_VECTOR = 6
-VECTOR_GROUPS = (0, 2)
+VECTOR_GROUPS = (0,)
 RUN = 4
 EPS = 1e-5
 
@@ -54,12 +54,13 @@ def tile_attentionfreetransformerencoder_pb_kernel(tc, x, yt, ln1_g, ln1_b, Wq, 
             nc.sync.dma_start(out=dst[:], in_=w.rearrange("(p j) n -> p j n", j=PACK))
 
         nc.vector.memset(bo_row[:], 0.0)
-        load_chunk(x_sb, x_view, 0)
+        for i in range(CHUNK_TILES):
+            nc.sync.dma_start(out=x_sb[0][:, i, :], in_=x_view[:, i, :])
         load_chunk(x_sb, x_view, 1)
         nc.sync.dma_start(out=bo_row[0:1, :], in_=bo.unsqueeze(0))
+        load_weight(wq_raw, Wq)
         for i, vec in enumerate((ln1_g, ln1_b, bq)):
             nc.sync.dma_start(out=vec_raw[:, i, 0:PACK], in_=vec.rearrange("(p j) -> p j", j=PACK))
-        load_weight(wq_raw, Wq)
         load_chunk(x_sb, x_view, 2)
         load_chunk(x_sb, x_view, 3)
         load_weight(wo_raw, Wo)
@@ -108,10 +109,11 @@ def tile_attentionfreetransformerencoder_pb_kernel(tc, x, yt, ln1_g, ln1_b, Wq, 
                 in_=planes[:].rearrange("p j (c i) -> p c j i", i=RUN),
             )
 
-        def regroup_wq(copy, grouped, planes):
-            copy(
-                out=grouped[:].rearrange("p (t m) j -> p t m j", t=PACK),
-                in_=planes[:].rearrange("p j (m t) -> p t m j", t=PACK),
+        def regroup_wq(half):
+            t = slice(half * PACK // 2, (half + 1) * PACK // 2)
+            nc.scalar.copy(
+                out=wq_grouped[:].rearrange("p (t m) j -> p t m j", t=PACK)[:, t],
+                in_=wq_raw[:].rearrange("p j (m t) -> p t m j", t=PACK)[:, t],
             )
 
         def quantise(grouped, codes, scales):
@@ -285,35 +287,30 @@ def tile_attentionfreetransformerencoder_pb_kernel(tc, x, yt, ln1_g, ln1_b, Wq, 
         bo_bank = psum.tile([P, D], F32, name="bo_bank", tag="o")
         nc.tensor.matmul(bo_bank[:], ones_bf16[:], bo_row[:], start=True, stop=True)
         nc.scalar.copy(out=bo_all[:], in_=bo_bank[:])
-        nc.scalar.copy(out=cols[:].rearrange("p (i j) -> p i j", j=PACK), in_=vec_raw[:, :, 0:PACK])
-        stats(1)
-        mean_shift(0, 1)
-        inverse_deviation(1, 1)
+        regroup_wq(0)
+        for c in range(1, 4):
+            stats(c)
+            mean_shift(c - 1, 1)
+            inverse_deviation(c, 1)
         normalise(0)
         transpose_x(0)
-        regroup_wq(nc.scalar.copy, wq_grouped, wq_raw)
-        stats(2)
-        stats(3)
-        mean_shift(1, 1)
-        inverse_deviation(2, 2)
+        regroup_wq(1)
+        nc.scalar.copy(out=cols[:].rearrange("p (i j) -> p i j", j=PACK), in_=vec_raw[:, :, 0:PACK])
         normalise(1)
         gain_shift(0)
         transpose_x(1)
-        regroup(nc.vector.tensor_copy, wo_grouped, wo_raw)
-        stats(4)
-        mean_shift(2, 2)
         normalise(2)
-        quantise(wq_grouped[:], wq_codes[:], wq_scales[:])
-        stats(5)
+        regroup(nc.vector.tensor_copy, wo_grouped, wo_raw)
+        mean_shift(3, 1)
+        stats(4)
         group_h(0)
+        quantise(wq_grouped[:], wq_codes[:], wq_scales[:])
         quantise_h(0)
         q_matmuls(0)
         transpose_yt(0)
-        inverse_deviation(4, 2)
+        stats(5)
         quantise(wo_grouped[:], wo_codes[:], wo_scales[:])
-        stats(6)
-        mean_shift(4, 2)
-        stats(7)
+        inverse_deviation(4, 2)
 
         for s in range(1, CHUNKS + 2):
             run(gain_shift, s)
@@ -327,16 +324,20 @@ def tile_attentionfreetransformerencoder_pb_kernel(tc, x, yt, ln1_g, ln1_b, Wq, 
             if s - 2 < CHUNKS - 1:
                 run(out_matmul, s - 2, 0)
                 run(out_matmul, s - 2, 1)
+            if s == 2:
+                mean_shift(6, 2)
             run(quantise_h, s)
             run(q_matmuls, s)
             run(transpose_yt, s)
             if s == 1:
-                inverse_deviation(6, 2)
+                stats(6)
+                mean_shift(4, 2)
+                stats(7)
             if s - 1 < RES_ON_VECTOR:
                 residual(s - 1)
-            run(product, s - 1, 0)
             if s == 1:
-                mean_shift(6, 2)
+                inverse_deviation(6, 2)
+            run(product, s - 1, 0)
             if s - 1 == CHUNKS - 1:
                 product(s - 1, 1)
                 quantise_y(s - 1, 0)

@@ -19,7 +19,7 @@ CHUNK_ROWS = CHUNK_TILES * P
 CHUNKS = TILES // CHUNK_TILES
 VEC_PAD = 16
 RES_ON_VECTOR = 6
-VECTOR_GROUPS = (0,)
+VECTOR_GROUPS = (0, 2, 4)
 RUN = 4
 EPS = 1e-5
 
@@ -314,8 +314,8 @@ def tile_attentionfreetransformerencoder_pb_kernel(tc, x, yt, ln1_g, ln1_b, Wq, 
 
         for s in range(1, CHUNKS + 2):
             run(gain_shift, s)
-            run(normalise, s + 2)
             run(group_h, s)
+            run(normalise, s + 2)
             run(sigmoid, s - 1)
             run(transpose_x, s + 1)
             if CHUNKS - 1 <= s <= CHUNKS:
@@ -324,6 +324,8 @@ def tile_attentionfreetransformerencoder_pb_kernel(tc, x, yt, ln1_g, ln1_b, Wq, 
             if s - 2 < CHUNKS - 1:
                 run(out_matmul, s - 2, 0)
                 run(out_matmul, s - 2, 1)
+            if 2 <= s <= RES_ON_VECTOR:
+                residual(s - 1)
             if s == 2:
                 mean_shift(6, 2)
             run(quantise_h, s)
@@ -333,9 +335,7 @@ def tile_attentionfreetransformerencoder_pb_kernel(tc, x, yt, ln1_g, ln1_b, Wq, 
                 stats(6)
                 mean_shift(4, 2)
                 stats(7)
-            if s - 1 < RES_ON_VECTOR:
-                residual(s - 1)
-            if s == 1:
+                residual(0)
                 inverse_deviation(6, 2)
             run(product, s - 1, 0)
             if s - 1 == CHUNKS - 1:

import concourse.mybir as mybir
from concourse.masks import make_identity

F32 = mybir.dt.float32
BF16 = mybir.dt.bfloat16
U32 = mybir.dt.uint32
U8 = mybir.dt.uint8
FP8X4 = mybir.dt.float8_e4m3fn_x4
ALU = mybir.AluOpType
ACT = mybir.ActivationFunctionType

P = 128
PACK = 4
D = P * PACK
ROWS = 2048
TILES = ROWS // P
CHUNK_TILES = 2
CHUNK_ROWS = CHUNK_TILES * P
CHUNKS = TILES // CHUNK_TILES
VEC_PAD = 16
RES_ON_VECTOR = 6
VECTOR_GROUPS = (0, 2, 4)
RUN = 4
EPS = 1e-5

FLOPS = 2 * 2 * ROWS * D * D


def tile_attentionfreetransformerencoder_pb_kernel(tc, x, yt, ln1_g, ln1_b, Wq, bq, Wo, bo, out):
    nc = tc.nc
    x_view = x.flatten_outer_dims().rearrange("(p t) d -> p t d", t=TILES)
    yt_view = yt.flatten_outer_dims().rearrange("(p t) d -> p t d", t=TILES)
    out_view = out.flatten_outer_dims().rearrange("(p t) d -> p t d", t=TILES)

    with (
        tc.tile_pool(name="consts", bufs=1) as consts,
        tc.tile_pool(name="resident", bufs=1) as resident,
        tc.tile_pool(name="work", bufs=3) as work,
        tc.psum_pool(name="psum", bufs=2) as psum,
        tc.manual_schedule(),
    ):
        x_sb = [resident.tile([P, CHUNK_TILES, D], BF16, name="x%d" % c) for c in range(CHUNKS)]
        yt_sb = [resident.tile([P, CHUNK_TILES, D], BF16, name="yt%d" % c) for c in range(CHUNKS)]
        wq_raw = consts.tile([P, PACK, D], BF16, name="wq_raw")
        wo_raw = consts.tile([P, PACK, D], BF16, name="wo_raw")
        vec_raw = consts.tile([P, 3, VEC_PAD], BF16, name="vec_raw")
        bo_row = consts.tile([P, D], BF16, name="bo_row")
        bo_all = consts.tile([P, D], F32, name="bo_all")

        def load_chunk(dst, view, c):
            nc.sync.dma_start(out=dst[c][:], in_=view[:, c * CHUNK_TILES : (c + 1) * CHUNK_TILES, :])

        def load_weight(dst, w):
            nc.sync.dma_start(out=dst[:], in_=w.rearrange("(p j) n -> p j n", j=PACK))

        nc.vector.memset(bo_row[:], 0.0)
        for i in range(CHUNK_TILES):
            nc.sync.dma_start(out=x_sb[0][:, i, :], in_=x_view[:, i, :])
        load_chunk(x_sb, x_view, 1)
        nc.sync.dma_start(out=bo_row[0:1, :], in_=bo.unsqueeze(0))
        load_weight(wq_raw, Wq)
        for i, vec in enumerate((ln1_g, ln1_b, bq)):
            nc.sync.dma_start(out=vec_raw[:, i, 0:PACK], in_=vec.rearrange("(p j) -> p j", j=PACK))
        load_chunk(x_sb, x_view, 2)
        load_chunk(x_sb, x_view, 3)
        load_weight(wo_raw, Wo)
        for c in range(4, CHUNKS):
            load_chunk(x_sb, x_view, c)
            load_chunk(yt_sb, yt_view, c - 4)
        for c in range(CHUNKS - 4, CHUNKS):
            load_chunk(yt_sb, yt_view, c)

        warm = consts.tile([P, 1], F32, name="warm")
        nc.vector.memset(warm[:], 0.0)
        warm_out = consts.tile([P, 1], F32, name="warm_out")
        nc.scalar.activation(out=warm_out[:], in_=warm[:], func=ACT.Sigmoid)

        ident_bf16 = consts.tile([P, P], BF16, name="ident_bf16")
        make_identity(nc, ident_bf16[:])
        ident_f32 = consts.tile([P, P], F32, name="ident_f32")
        make_identity(nc, ident_f32[:])
        ones_bf16 = consts.tile([P, P], BF16, name="ones_bf16")
        nc.gpsimd.memset(ones_bf16[:], 1.0)
        neg_half = consts.tile([P, TILES], F32, name="neg_half")
        nc.gpsimd.memset(neg_half[:], -0.5)

        wq_grouped = consts.tile([P, D, PACK], BF16, name="wq_grouped", align_bytes=64)
        wo_grouped = consts.tile([P, D, PACK], BF16, name="wo_grouped", align_bytes=64)
        wq_codes = consts.tile([P, D], U32, name="wq_codes", align_bytes=64)
        wq_scales = consts.tile([P, D], U8, name="wq_scales", align_bytes=64)
        wo_codes = consts.tile([P, D], U32, name="wo_codes", align_bytes=64)
        wo_scales = consts.tile([P, D], U8, name="wo_scales", align_bytes=64)
        cols = consts.tile([P, 3 * PACK], F32, name="cols")
        g_col = cols[:, 0:PACK]
        b_col = cols[:, PACK : 2 * PACK]
        bq_col = cols[:, 2 * PACK : 3 * PACK]

        mean_var = consts.tile([P, TILES, 2], F32, name="mean_var")
        var_eps = consts.tile([P, TILES], F32, name="var_eps")
        rstd = consts.tile([P, TILES], F32, name="rstd")
        shift = consts.tile([P, TILES], F32, name="shift")

        xn, xnT, hT, h_grouped, h_codes, h_scales = {}, {}, {}, {}, {}, {}
        qT, gate, ytT, y_grouped, y_codes, y_scales, o, res, res_banks = {}, {}, {}, {}, {}, {}, {}, {}, {}

        def regroup(copy, grouped, planes):
            copy(
                out=grouped[:].rearrange("p (c i) j -> p c j i", i=RUN),
                in_=planes[:].rearrange("p j (c i) -> p c j i", i=RUN),
            )

        def regroup_wq(half):
            t = slice(half * PACK // 2, (half + 1) * PACK // 2)
            nc.scalar.copy(
                out=wq_grouped[:].rearrange("p (t m) j -> p t m j", t=PACK)[:, t],
                in_=wq_raw[:].rearrange("p j (m t) -> p t m j", t=PACK)[:, t],
            )

        def quantise(grouped, codes, scales):
            nc.vector.quantize_mx(out=codes.bitcast(FP8X4), scales=scales, in_=grouped.rearrange("p w j -> p (w j)"))

        def part(c, i):
            return slice(i * P, (i + 1) * P) if c == CHUNKS - 1 else slice(0, CHUNK_ROWS)

        def stats(c):
            bn = resident.tile([P, CHUNK_TILES, 6], F32, name="bn%d" % c)
            for i in range(CHUNK_TILES):
                nc.vector.bn_stats(out=bn[:, i, :], in_=x_sb[c][:, i, :])
            for i in range(CHUNK_TILES):
                nc.vector.bn_aggr(out=mean_var[:, c * CHUNK_TILES + i, :], in_=bn[:, i, :])

        def tiles_of(first, count):
            return slice(first * CHUNK_TILES, (first + count) * CHUNK_TILES)

        def inverse_deviation(first, count):
            t = tiles_of(first, count)
            nc.vector.tensor_scalar(out=var_eps[:, t], in0=mean_var[:, t, 1], scalar1=EPS, scalar2=None, op0=ALU.add)
            nc.gpsimd.tensor_tensor(out=rstd[:, t], in0=var_eps[:, t], in1=neg_half[:, t], op=ALU.pow)

        def mean_shift(first, count):
            t = tiles_of(first, count)
            nc.vector.scalar_tensor_tensor(
                out=shift[:, t], in0=mean_var[:, t, 0], scalar=-1.0, in1=rstd[:, t], op0=ALU.mult, op1=ALU.mult
            )

        def normalise(c):
            xn[c] = work.tile([P, CHUNK_TILES, PACK, P], F32, name="xn")
            for i in range(CHUNK_TILES):
                nc.scalar.activation(
                    out=xn[c][:, i, :, :],
                    in_=x_sb[c][:, i, :].rearrange("p (m j) -> p j m", j=PACK),
                    func=ACT.Identity,
                    scale=rstd[:, c * CHUNK_TILES + i : c * CHUNK_TILES + i + 1],
                    bias=shift[:, c * CHUNK_TILES + i : c * CHUNK_TILES + i + 1],
                )

        def transpose_x(c):
            xnT[c] = []
            for b in range(2):
                bank = psum.tile([P, 2, CHUNK_ROWS], F32, name="xnT")
                for jj in range(2):
                    j = 2 * b + jj
                    for i in range(CHUNK_TILES):
                        nc.tensor.transpose(
                            bank[:, jj, i * P : (i + 1) * P], xn[c][:, i, j, :], ident_f32[:]
                        )
                xnT[c].append(bank)

        def gain_shift(c):
            hT[c] = work.tile([P, PACK, CHUNK_ROWS], BF16, name="hT")
            for j in range(PACK):
                nc.scalar.activation(
                    out=hT[c][:, j, :],
                    in_=xnT[c][j // 2][:, j % 2, :],
                    func=ACT.Identity,
                    scale=g_col[:, j : j + 1],
                    bias=b_col[:, j : j + 1],
                )

        def group_h(c):
            h_grouped[c] = work.tile([P, CHUNK_ROWS, PACK], BF16, name="h_grouped", align_bytes=64)
            regroup(nc.vector.tensor_copy if c in VECTOR_GROUPS else nc.scalar.copy, h_grouped[c], hT[c])

        def quantise_h(c):
            h_codes[c] = work.tile([P, CHUNK_ROWS], U32, name="h_codes", align_bytes=64)
            h_scales[c] = work.tile([P, CHUNK_ROWS], U8, name="h_scales", align_bytes=64)
            quantise(h_grouped[c][:], h_codes[c][:], h_scales[c][:])

        def q_matmuls(c):
            qT[c] = []
            for b in range(2):
                bank = psum.tile([P, 2, CHUNK_ROWS], F32, name="qT")
                for jj in range(2):
                    j = 2 * b + jj
                    nc.tensor.matmul_mx(
                        out=bank[:, jj, :],
                        lhsT=wq_codes[:, j * P : (j + 1) * P].bitcast(FP8X4),
                        lhsT_scale=wq_scales[:, j * P : (j + 1) * P],
                        rhs=h_codes[c][:].bitcast(FP8X4),
                        rhs_scale=h_scales[c][:],
                        start=True,
                        stop=True,
                    )
                qT[c].append(bank)

        def sigmoid(c):
            gate[c] = work.tile([P, PACK, CHUNK_ROWS], F32, name="gate")
            for j in range(PACK):
                nc.scalar.activation(
                    out=gate[c][:, j, :],
                    in_=qT[c][j // 2][:, j % 2, :],
                    func=ACT.Sigmoid,
                    bias=bq_col[:, j : j + 1],
                )

        def transpose_yt(c):
            ytT[c] = psum.tile([P, PACK, CHUNK_ROWS], BF16, name="ytT")
            for j in range(PACK):
                for i in range(CHUNK_TILES):
                    nc.tensor.transpose(ytT[c][:, j, i * P : (i + 1) * P], yt_sb[c][:, i, j::PACK], ident_bf16[:])

        def product(c, i):
            if i == 0:
                y_grouped[c] = work.tile([P, CHUNK_ROWS, PACK], BF16, name="y_grouped", align_bytes=64)
            w = part(c, i)
            nc.vector.tensor_tensor(
                out=y_grouped[c][:, w, :].rearrange("p (c i) j -> p c j i", i=RUN),
                in0=ytT[c][:, :, w].rearrange("p j (c i) -> p c j i", i=RUN),
                in1=gate[c][:, :, w].rearrange("p j (c i) -> p c j i", i=RUN),
                op=ALU.mult,
            )

        def quantise_y(c, i):
            if i == 0:
                y_codes[c] = work.tile([P, CHUNK_ROWS], U32, name="y_codes", align_bytes=64)
                y_scales[c] = work.tile([P, CHUNK_ROWS], U8, name="y_scales", align_bytes=64)
            w = part(c, i)
            quantise(y_grouped[c][:, w, :], y_codes[c][:, w], y_scales[c][:, w])

        def out_matmul(c, i):
            if i == 0:
                o[c] = []
            bank = psum.tile([P, D], F32, name="o")
            nc.tensor.matmul_mx(
                out=bank[:],
                lhsT=y_codes[c][:, i * P : (i + 1) * P].bitcast(FP8X4),
                lhsT_scale=y_scales[c][:, i * P : (i + 1) * P],
                rhs=wo_codes[:].bitcast(FP8X4),
                rhs_scale=wo_scales[:],
                start=True,
                stop=True,
            )
            o[c].append(bank)

        def residual_on_tensor(c):
            res_banks[c] = []
            for i in range(CHUNK_TILES):
                bank = psum.tile([P, D], F32, name="res_bank", tag="xnT")
                nc.tensor.matmul(bank[:], ones_bf16[:], bo_row[:], start=True, stop=False)
                nc.tensor.matmul(bank[:], ident_bf16[:], x_sb[c][:, i, :], start=False, stop=True)
                res_banks[c].append(bank)

        def copy_residual(c):
            res[c] = resident.tile([P, CHUNK_TILES, D], F32, name="res%d" % c)
            for i in range(CHUNK_TILES):
                nc.scalar.copy(out=res[c][:, i, :], in_=res_banks[c][i][:])

        def residual(c):
            res[c] = resident.tile([P, CHUNK_TILES, D], F32, name="res%d" % c)
            nc.vector.tensor_tensor(
                out=res[c][:],
                in0=x_sb[c][:],
                in1=bo_all[:].unsqueeze(1).to_broadcast([P, CHUNK_TILES, D]),
                op=ALU.add,
            )

        def add_store(c, i):
            nc.vector.tensor_tensor(out=res[c][:, i, :], in0=o[c][i][:], in1=res[c][:, i, :], op=ALU.add)
            nc.sync.dma_start(out=out_view[:, c * CHUNK_TILES + i, :], in_=res[c][:, i, :])

        def run(stage, c, *i):
            if 0 <= c < CHUNKS:
                stage(c, *i)

        stats(0)
        inverse_deviation(0, 1)
        bo_bank = psum.tile([P, D], F32, name="bo_bank", tag="o")
        nc.tensor.matmul(bo_bank[:], ones_bf16[:], bo_row[:], start=True, stop=True)
        nc.scalar.copy(out=bo_all[:], in_=bo_bank[:])
        regroup_wq(0)
        for c in range(1, 4):
            stats(c)
            mean_shift(c - 1, 1)
            inverse_deviation(c, 1)
        normalise(0)
        transpose_x(0)
        regroup_wq(1)
        nc.scalar.copy(out=cols[:].rearrange("p (i j) -> p i j", j=PACK), in_=vec_raw[:, :, 0:PACK])
        normalise(1)
        gain_shift(0)
        transpose_x(1)
        normalise(2)
        regroup(nc.vector.tensor_copy, wo_grouped, wo_raw)
        mean_shift(3, 1)
        stats(4)
        group_h(0)
        quantise(wq_grouped[:], wq_codes[:], wq_scales[:])
        quantise_h(0)
        q_matmuls(0)
        transpose_yt(0)
        stats(5)
        quantise(wo_grouped[:], wo_codes[:], wo_scales[:])
        inverse_deviation(4, 2)

        for s in range(1, CHUNKS + 2):
            run(gain_shift, s)
            run(group_h, s)
            run(normalise, s + 2)
            run(sigmoid, s - 1)
            run(transpose_x, s + 1)
            if CHUNKS - 1 <= s <= CHUNKS:
                residual_on_tensor(s - 1)
                copy_residual(s - 1)
            if s - 2 < CHUNKS - 1:
                run(out_matmul, s - 2, 0)
                run(out_matmul, s - 2, 1)
            if 2 <= s <= RES_ON_VECTOR:
                residual(s - 1)
            if s == 2:
                mean_shift(6, 2)
            run(quantise_h, s)
            run(q_matmuls, s)
            run(transpose_yt, s)
            if s == 1:
                stats(6)
                mean_shift(4, 2)
                stats(7)
                residual(0)
                inverse_deviation(6, 2)
            run(product, s - 1, 0)
            if s - 1 == CHUNKS - 1:
                product(s - 1, 1)
                quantise_y(s - 1, 0)
                out_matmul(s - 1, 0)
            run(add_store, s - 2, 0)
            run(add_store, s - 2, 1)
            if s - 1 == CHUNKS - 1:
                quantise_y(s - 1, 1)
                out_matmul(s - 1, 1)
            else:
                run(quantise_y, s - 1, 0)
